import numpy as np
import ml_dtypes


def mxq(x, axis, fmt="e4m3"):
    dtype, down = {"e4m3": (ml_dtypes.float8_e4m3fn, 7), "e5m2": (ml_dtypes.float8_e5m2, 14)}[fmt]
    v = np.moveaxis(np.asarray(x, np.float32).astype(ml_dtypes.bfloat16).astype(np.float64), axis, -1)
    blocks = v.reshape(v.shape[:-1] + (-1, 32))
    amax = np.abs(blocks).max(-1, keepdims=True)
    byte = np.maximum(np.where(amax > 0, np.frexp(amax)[1] - 1 + 127, 0) - down, 1)
    scale = np.exp2(byte - 127.0)
    codes = (blocks / scale).astype(np.float32).astype(dtype).astype(np.float64)
    return np.moveaxis((codes * scale).reshape(v.shape), -1, axis)


WIDE = False


def mx_kscale(k):
    if not WIDE:
        return np.ones(k)
    levels = np.array([10, -10, 5, -5, 0])
    a = np.random.permutation(np.resize(levels, k // 512 * 4)).reshape(k // 512, 4)
    idx = np.arange(k)
    return np.exp2(a[idx // 512, idx % 128 // 32])


BF16 = ml_dtypes.bfloat16


def bf(x):
    return np.asarray(x, np.float32).astype(BF16)


def f64(x):
    return np.asarray(x).astype(np.float64)


B, D_IN, H, D_OUT, DEPTH, Q = 128, 1024, 1024, 128, 3, 2


def quantum_probs(qw):
    n = qw.shape[1]
    s0r, s0i, s1r, s1i = np.ones(n), np.zeros(n), np.zeros(n), np.zeros(n)
    for d in range(qw.shape[0]):
        th = qw[d, :, 0, 0]
        ph = qw[d, :, 1, 1]
        c, s = np.cos(th), np.sin(th)
        n0r, n0i = c * s0r - s * s1r, c * s0i - s * s1i
        n1r, n1i = s * s0r + c * s1r, s * s0i + c * s1i
        cp, sp = np.cos(ph), np.sin(ph)
        s0r, s0i = n0r, n0i
        s1r, s1i = n1r * cp - n1i * sp, n1r * sp + n1i * cp
    return s0r * s0r + s0i * s0i


def setup_inputs():
    s = mx_kscale(H)
    return {"h3": bf(np.maximum(np.random.standard_normal((B, H)), 0.0) * s),
            "q2_qw": bf(np.random.standard_normal((DEPTH, H, Q, Q))),
            "q2_cw": bf(np.random.standard_normal((H, H)) * 1.4 / np.sqrt(H) / s[:, None]),
            "q2_cb": bf(np.random.standard_normal(H) * 0.3),
            "w3": bf(np.random.standard_normal((H, D_OUT)) * 1.4 / np.sqrt(H)),
            "b3": bf(np.random.standard_normal(D_OUT) * 0.3)}


def reference(h3, q2_qw, q2_cw, q2_cb, w3, b3):
    h4 = np.tanh((mxq(f64(h3), 1, "e4m3") @ mxq(f64(q2_cw), 0, "e4m3")) + f64(q2_cb) + quantum_probs(f64(q2_qw))[None, :])
    return np.maximum((mxq(h4, 1, "e4m3") @ mxq(f64(w3), 0, "e4m3")) + f64(b3), 0.0)

@@ -1,0 +1,287 @@
+import math
+from contextlib import ExitStack
+
+import concourse.mybir as mybir
+from concourse.masks import make_identity
+
+F32 = mybir.dt.float32
+BF16 = mybir.dt.bfloat16
+I32 = mybir.dt.int32
+U32 = mybir.dt.uint32
+U8 = mybir.dt.uint8
+FP8X4 = mybir.dt.float8_e4m3fn_x4
+ACT = mybir.ActivationFunctionType
+ALU = mybir.AluOpType
+
+P = 128
+PACK = 4
+K_PASS = P * PACK
+B, H, D_OUT = 128, 1024, 128
+PASSES = H // K_PASS
+UNITS = K_PASS // P
+BLOCKS = H // P
+RUN = 4
+
+CHUNKS = PASSES * PASSES
+HALF = K_PASS // 2
+
+TH0, TH1, TH2, PH0, PH1 = 0, 1, 2, 4, 5
+SLOTS = 8
+SIN, COS = 0, 1
+
+FLOPS = 2 * B * H * H + 2 * B * H * D_OUT
+
+
+def regroup(copy, grouped, rows):
+    copy(
+        out=grouped.rearrange("p (c i) t -> p c t i", i=RUN),
+        in_=rows.rearrange("p t (c i) -> p c t i", i=RUN),
+    )
+
+
+def twice(column):
+    return column.unsqueeze(1).to_broadcast([P, 2, BLOCKS])
+
+
+def tile_quantumneuralnetwork_pb_s_kernel(tc, h3, q2_qw, q2_cw, q2_cb, w3, b3, out):
+    nc = tc.nc
+    lower, upper = slice(0, HALF), slice(HALF, K_PASS)
+    with ExitStack() as ctx:
+        keep = ctx.enter_context(tc.tile_pool(name="keep", bufs=1))
+        psum = ctx.enter_context(tc.psum_pool(name="psum", bufs=1))
+        acc_pool = ctx.enter_context(tc.psum_pool(name="acc_pool", bufs=UNITS))
+        ctx.enter_context(tc.manual_schedule())
+
+        small_rows = keep.tile([P, K_PASS + P], BF16)
+        nc.gpsimd.memset(small_rows[:].bitcast(F32), 0.0)
+        warm = keep.tile([P, 1], F32)
+        nc.vector.memset(warm[:], 0.0)
+        phase = keep.tile([P, 2, SLOTS * BLOCKS], F32)
+        nc.vector.memset(phase[:, SIN, :], 0.0)
+        nc.vector.memset(phase[:, COS, :], 0.25)
+        ident_bf = keep.tile([P, P], BF16)
+        make_identity(nc, ident_bf[:])
+        ident_f32 = keep.tile([P, P], F32)
+        make_identity(nc, ident_f32[:])
+
+        nc.sync.dma_start(
+            out=small_rows[0 : 3 * BLOCKS, 0:K_PASS],
+            in_=q2_qw.rearrange("d (n j) a b -> (d n) (j a b)", j=P),
+        )
+        nc.sync.dma_start(
+            out=small_rows[0:BLOCKS, K_PASS : K_PASS + P],
+            in_=q2_cb.rearrange("(n j) -> n j", j=P),
+        )
+        nc.scalar.activation(out=warm[:], in_=warm[:], func=ACT.Silu)
+
+        cw_rows = [
+            keep.tile([P, PACK, K_PASS], BF16, name="cw_rows_%d" % i) for i in range(CHUNKS)
+        ]
+
+        def load_chunk(i):
+            g, c = divmod(i, PASSES)
+            nc.sync.dma_start(
+                out=cw_rows[i][:],
+                in_=q2_cw[
+                    c * K_PASS : (c + 1) * K_PASS, g * K_PASS : (g + 1) * K_PASS
+                ].rearrange("(p t) w -> p t w", t=PACK),
+            )
+
+        h3_rows = keep.tile([P, H], BF16)
+        load_chunk(0)
+        nc.sync.dma_start(out=h3_rows[:], in_=h3)
+        for i in range(1, CHUNKS):
+            load_chunk(i)
+        w3_rows = keep.tile([P, PASSES, PACK, D_OUT], BF16)
+        nc.sync.dma_start(
+            out=w3_rows[:].rearrange("p g t n -> p (g t) n"),
+            in_=w3.rearrange("(s p) n -> p s n", p=P),
+        )
+        b3_all = keep.tile([P, D_OUT], BF16)
+        nc.sync.dma_start(out=b3_all[:], in_=b3.partition_broadcast(P))
+
+        cw_grouped = [
+            keep.tile([P, K_PASS, PACK], BF16, align_bytes=64, name="cw_grouped_%d" % i)
+            for i in range(CHUNKS)
+        ]
+        cw_codes = keep.tile([P, CHUNKS, K_PASS], U32, align_bytes=64)
+        cw_scales = keep.tile([P, CHUNKS, K_PASS], U8, align_bytes=64)
+
+        def regroup_chunk(i):
+            regroup(nc.vector.tensor_copy, cw_grouped[i][:, lower, :], cw_rows[i][:, :, lower])
+            regroup(nc.scalar.copy, cw_grouped[i][:, upper, :], cw_rows[i][:, :, upper])
+
+        def quantise_chunk(i, half):
+            nc.vector.quantize_mx(
+                out=cw_codes[:, i, half].bitcast(FP8X4),
+                scales=cw_scales[:, i, half],
+                in_=cw_grouped[i][:, half, :].rearrange("p w t -> p (w t)"),
+            )
+
+        theta = small_rows[:, 0:K_PASS:4]
+        phi = small_rows[:, 3:K_PASS:4]
+        first_rows = ident_bf[:, 0 : 4 * BLOCKS]
+        small_t = psum.tile([P, 3, 4 * BLOCKS], F32)
+        nc.tensor.matmul(out=small_t[:, 0, :], lhsT=theta, rhs=first_rows, start=True, stop=False)
+        nc.tensor.matmul(out=small_t[:, 0, :], lhsT=theta, rhs=first_rows, start=False, stop=True)
+        nc.tensor.matmul(out=small_t[:, 1, :], lhsT=phi, rhs=first_rows, start=True, stop=True)
+        nc.tensor.matmul(
+            out=small_t[:, 2, :], lhsT=small_rows[:, K_PASS : K_PASS + P], rhs=first_rows,
+            start=True, stop=True,
+        )
+        angles = small_t[:, 0:2, :].rearrange("p a r -> p (a r)")
+
+        turns = keep.tile([P, 2, SLOTS * BLOCKS], F32)
+        nc.vector.scalar_tensor_tensor(
+            out=turns[:],
+            in0=angles.unsqueeze(1).to_broadcast([P, 2, SLOTS * BLOCKS]),
+            scalar=1.0 / (2.0 * math.pi),
+            in1=phase[:],
+            op0=ALU.mult,
+            op1=ALU.add,
+        )
+        whole = keep.tile([P, 2, SLOTS * BLOCKS], I32)
+        nc.vector.tensor_copy(out=whole[:], in_=turns[:])
+        nc.vector.tensor_tensor(out=turns[:], in0=turns[:], in1=whole[:], op=ALU.subtract)
+        cb_half = keep.tile([P, BLOCKS], F32)
+        nc.vector.tensor_scalar(
+            out=cb_half[:], in0=small_t[:, 2, 0:BLOCKS], scalar1=0.5, scalar2=None, op0=ALU.add
+        )
+
+        regroup_chunk(0)
+
+        trig = keep.tile([P, 2, SLOTS, BLOCKS], F32)
+        nc.scalar.activation(
+            out=trig[:].rearrange("p f a n -> p f (a n)"), in_=turns[:], func=ACT.Sin,
+            scale=2.0 * math.pi,
+        )
+
+        def product(name, in0, in1):
+            pair = keep.tile([P, 2, BLOCKS], F32, name=name)
+            nc.vector.tensor_tensor(out=pair[:], in0=in0, in1=in1, op=ALU.mult)
+            return pair
+
+        yx = product("yx", trig[:, :, PH0, :], twice(trig[:, SIN, TH0, :]))
+        z_part = product("z_part", trig[:, :, TH1, :], twice(trig[:, COS, TH0, :]))
+
+        h3_words = h3_rows[:].bitcast(F32)
+        h3_t = psum.tile([P, PASSES, 2, B], F32)
+        for c in range(PASSES):
+            for u in range(2):
+                nc.tensor.transpose(
+                    h3_t[:, c, u, :],
+                    h3_words[:, c * 2 * P + u : (c + 1) * 2 * P : 2],
+                    ident_f32[:],
+                )
+        h3_grouped = keep.tile([P, PASSES, B, 2], F32, align_bytes=64)
+        nc.scalar.copy(out=h3_grouped[:], in_=h3_t[:].rearrange("p c u b -> p c b u"))
+        h3_codes = keep.tile([P, PASSES, B], U32, align_bytes=64)
+        h3_scales = keep.tile([P, PASSES, B], U8, align_bytes=64)
+
+        regroup_chunk(1)
+        x_part = product("x_part", trig[:, :, TH1, :], twice(yx[:, 1, :]))
+        quantise_chunk(0, lower)
+        xz = keep.tile([P, 2, BLOCKS], F32)
+        nc.vector.tensor_tensor(
+            out=yx[:, 1, :], in0=x_part[:, COS, :], in1=z_part[:, SIN, :], op=ALU.add
+        )
+        nc.vector.tensor_tensor(
+            out=xz[:, 1, :], in0=z_part[:, COS, :], in1=x_part[:, SIN, :], op=ALU.subtract
+        )
+        quantise_chunk(0, upper)
+        yx_part = product("yx_part", yx[:], trig[:, :, PH1, :])
+        nc.vector.quantize_mx(
+            out=h3_codes[:].rearrange("p c b -> p (c b)").bitcast(FP8X4),
+            scales=h3_scales[:].rearrange("p c b -> p (c b)"),
+            in_=h3_grouped[:].rearrange("p c b u -> p (c b u)").bitcast(BF16),
+        )
+        nc.vector.tensor_tensor(
+            out=xz[:, 0, :], in0=yx_part[:, 1, :], in1=yx_part[:, 0, :], op=ALU.subtract
+        )
+        regroup_chunk(2)
+        xz_part = product("xz_part", xz[:], trig[:, :, TH2, :])
+        quantise_chunk(1, lower)
+        z_last = keep.tile([P, BLOCKS], F32)
+        nc.vector.tensor_tensor(
+            out=z_last[:], in0=xz_part[:, 1, :], in1=xz_part[:, 0, :], op=ALU.subtract
+        )
+        quantise_chunk(1, upper)
+        bias = keep.tile([P, BLOCKS], F32)
+        nc.vector.scalar_tensor_tensor(
+            out=bias[:], in0=z_last[:], scalar=0.5, in1=cb_half[:], op0=ALU.mult, op1=ALU.add
+        )
+        regroup_chunk(3)
+
+        h4_t = [keep.tile([P, PACK, B], BF16, name="h4_t_%d" % g) for g in range(PASSES)]
+
+        def first_product(g):
+            for t in range(UNITS):
+                units = slice(t * P, (t + 1) * P)
+                acc = acc_pool.tile([P, B], F32)
+                for c in range(PASSES):
+                    nc.tensor.matmul_mx(
+                        out=acc[:],
+                        lhsT=cw_codes[:, g * PASSES + c, units].bitcast(FP8X4),
+                        lhsT_scale=cw_scales[:, g * PASSES + c, units],
+                        rhs=h3_codes[:, c, :].bitcast(FP8X4),
+                        rhs_scale=h3_scales[:, c, :],
+                        start=(c == 0),
+                        stop=(c == PASSES - 1),
+                    )
+                n = g * UNITS + t
+                nc.scalar.activation(
+                    out=h4_t[g][:, t, :], in_=acc[:], func=ACT.Tanh, bias=bias[:, n : n + 1]
+                )
+
+        first_product(0)
+        for i in range(PASSES, CHUNKS):
+            quantise_chunk(i, lower)
+            quantise_chunk(i, upper)
+        first_product(1)
+
+        w3_grouped = keep.tile([P, PASSES, D_OUT, PACK], BF16, align_bytes=64)
+        w3_codes = keep.tile([P, PASSES, D_OUT], U32, align_bytes=64)
+        w3_scales = keep.tile([P, PASSES, D_OUT], U8, align_bytes=64)
+        h4_grouped = keep.tile([P, PASSES, B, PACK], BF16, align_bytes=64)
+        h4_codes = keep.tile([P, PASSES, B], U32, align_bytes=64)
+        h4_scales = keep.tile([P, PASSES, B], U8, align_bytes=64)
+        out_acc = psum.tile([B, D_OUT], F32)
+
+        def quantise_h4(g):
+            nc.vector.quantize_mx(
+                out=h4_codes[:, g, :].bitcast(FP8X4),
+                scales=h4_scales[:, g, :],
+                in_=h4_grouped[:, g, :, :].rearrange("p b t -> p (b t)"),
+            )
+
+        def second_product(g):
+            nc.tensor.matmul_mx(
+                out=out_acc[:],
+                lhsT=h4_codes[:, g, :].bitcast(FP8X4),
+                lhsT_scale=h4_scales[:, g, :],
+                rhs=w3_codes[:, g, :].bitcast(FP8X4),
+                rhs_scale=w3_scales[:, g, :],
+                start=(g == 0),
+                stop=(g == PASSES - 1),
+            )
+
+        for g in range(PASSES):
+            regroup(nc.vector.tensor_copy, w3_grouped[:, g, :, :], w3_rows[:, g, :, :])
+        regroup(nc.vector.tensor_copy, h4_grouped[:, 0, :, :], h4_t[0][:])
+        nc.vector.quantize_mx(
+            out=w3_codes[:].rearrange("p g n -> p (g n)").bitcast(FP8X4),
+            scales=w3_scales[:].rearrange("p g n -> p (g n)"),
+            in_=w3_grouped[:].rearrange("p g n t -> p (g n t)"),
+        )
+        quantise_h4(0)
+        second_product(0)
+        regroup(nc.vector.tensor_copy, h4_grouped[:, 1, :, :], h4_t[1][:])
+        quantise_h4(1)
+        second_product(1)
+
+        result = keep.tile([B, D_OUT], F32)
+        nc.vector.tensor_tensor(out=result[:], in0=out_acc[:], in1=b3_all[:], op=ALU.add)
+        nc.vector.tensor_scalar(
+            out=result[:], in0=result[:], scalar1=0.0, scalar2=None, op0=ALU.max
+        )
+        nc.sync.dma_start(out=out, in_=result[:])

@@ -16,7 +16,7 @@ ALU = mybir.AluOpType
 P = 128
 PACK = 4
 K_PASS = P * PACK
-B, H, D_OUT = 128, 1024, 128
+B, H, D_OUT, DEPTH = 128, 1024, 128, 3
 PASSES = H // K_PASS
 UNITS = K_PASS // P
 BLOCKS = H // P
@@ -54,31 +54,32 @@ def tile_quantumneuralnetwork_pb_s_kernel(tc, h3, q2_qw, q2_cw, q2_cb, w3, b3, o
 
         small_rows = keep.tile([P, K_PASS + P], BF16)
         nc.gpsimd.memset(small_rows[:].bitcast(F32), 0.0)
-        warm = keep.tile([P, 1], F32)
-        nc.vector.memset(warm[:], 0.0)
+        ident_f32 = keep.tile([P, P], F32)
+        make_identity(nc, ident_f32[:])
+        ident_bf = keep.tile([P, P], BF16)
+        make_identity(nc, ident_bf[:])
         phase = keep.tile([P, 2, SLOTS * BLOCKS], F32)
         nc.vector.memset(phase[:, SIN, :], 0.0)
         nc.vector.memset(phase[:, COS, :], 0.25)
-        ident_bf = keep.tile([P, P], BF16)
-        make_identity(nc, ident_bf[:])
-        ident_f32 = keep.tile([P, P], F32)
-        make_identity(nc, ident_f32[:])
+        warm = keep.tile([P, 1], F32)
+        nc.vector.memset(warm[:], 0.0)
+        nc.scalar.activation(out=warm[:], in_=warm[:], func=ACT.Silu)
 
-        nc.sync.dma_start(
-            out=small_rows[0 : 3 * BLOCKS, 0:K_PASS],
-            in_=q2_qw.rearrange("d (n j) a b -> (d n) (j a b)", j=P),
-        )
+        h3_rows = keep.tile([P, H], BF16)
+        nc.sync.dma_start(out=h3_rows[:], in_=h3)
+        for d in range(DEPTH):
+            nc.sync.dma_start(
+                out=small_rows[d * BLOCKS : (d + 1) * BLOCKS, 0:K_PASS],
+                in_=q2_qw[d].rearrange("(n j) a b -> n (j a b)", j=P),
+            )
         nc.sync.dma_start(
             out=small_rows[0:BLOCKS, K_PASS : K_PASS + P],
             in_=q2_cb.rearrange("(n j) -> n j", j=P),
         )
-        nc.scalar.activation(out=warm[:], in_=warm[:], func=ACT.Silu)
-
         cw_rows = [
             keep.tile([P, PACK, K_PASS], BF16, name="cw_rows_%d" % i) for i in range(CHUNKS)
         ]
-
-        def load_chunk(i):
+        for i in range(CHUNKS):
             g, c = divmod(i, PASSES)
             nc.sync.dma_start(
                 out=cw_rows[i][:],
@@ -86,12 +87,6 @@ def tile_quantumneuralnetwork_pb_s_kernel(tc, h3, q2_qw, q2_cw, q2_cb, w3, b3, o
                     c * K_PASS : (c + 1) * K_PASS, g * K_PASS : (g + 1) * K_PASS
                 ].rearrange("(p t) w -> p t w", t=PACK),
             )
-
-        h3_rows = keep.tile([P, H], BF16)
-        load_chunk(0)
-        nc.sync.dma_start(out=h3_rows[:], in_=h3)
-        for i in range(1, CHUNKS):
-            load_chunk(i)
         w3_rows = keep.tile([P, PASSES, PACK, D_OUT], BF16)
         nc.sync.dma_start(
             out=w3_rows[:].rearrange("p g t n -> p (g t) n"),
@@ -118,6 +113,20 @@ def tile_quantumneuralnetwork_pb_s_kernel(tc, h3, q2_qw, q2_cw, q2_cb, w3, b3, o
                 in_=cw_grouped[i][:, half, :].rearrange("p w t -> p (w t)"),
             )
 
+        h3_words = h3_rows[:].bitcast(F32)
+        h3_t = psum.tile([P, PASSES, 2, B], F32)
+        for c in range(PASSES):
+            for u in range(2):
+                nc.tensor.transpose(
+                    h3_t[:, c, u, :],
+                    h3_words[:, c * 2 * P + u : (c + 1) * 2 * P : 2],
+                    ident_f32[:],
+                )
+        h3_grouped = keep.tile([P, PASSES, B, 2], F32, align_bytes=64)
+        nc.scalar.copy(out=h3_grouped[:], in_=h3_t[:].rearrange("p c u b -> p c b u"))
+        h3_codes = keep.tile([P, PASSES, B], U32, align_bytes=64)
+        h3_scales = keep.tile([P, PASSES, B], U8, align_bytes=64)
+
         theta = small_rows[:, 0:K_PASS:4]
         phi = small_rows[:, 3:K_PASS:4]
         first_rows = ident_bf[:, 0 : 4 * BLOCKS]
@@ -140,21 +149,26 @@ def tile_quantumneuralnetwork_pb_s_kernel(tc, h3, q2_qw, q2_cw, q2_cb, w3, b3, o
             op0=ALU.mult,
             op1=ALU.add,
         )
-        whole = keep.tile([P, 2, SLOTS * BLOCKS], I32)
-        nc.vector.tensor_copy(out=whole[:], in_=turns[:])
-        nc.vector.tensor_tensor(out=turns[:], in0=turns[:], in1=whole[:], op=ALU.subtract)
         cb_half = keep.tile([P, BLOCKS], F32)
         nc.vector.tensor_scalar(
             out=cb_half[:], in0=small_t[:, 2, 0:BLOCKS], scalar1=0.5, scalar2=None, op0=ALU.add
         )
-
         regroup_chunk(0)
-
+        whole = keep.tile([P, 2, SLOTS * BLOCKS], I32)
+        nc.vector.tensor_copy(out=whole[:], in_=turns[:])
+        nc.vector.quantize_mx(
+            out=h3_codes[:].rearrange("p c b -> p (c b)").bitcast(FP8X4),
+            scales=h3_scales[:].rearrange("p c b -> p (c b)"),
+            in_=h3_grouped[:].rearrange("p c b u -> p (c b u)").bitcast(BF16),
+        )
+        nc.vector.tensor_tensor(out=turns[:], in0=turns[:], in1=whole[:], op=ALU.subtract)
         trig = keep.tile([P, 2, SLOTS, BLOCKS], F32)
         nc.scalar.activation(
             out=trig[:].rearrange("p f a n -> p f (a n)"), in_=turns[:], func=ACT.Sin,
             scale=2.0 * math.pi,
         )
+        quantise_chunk(0, lower)
+        regroup_chunk(1)
 
         def product(name, in0, in1):
             pair = keep.tile([P, 2, BLOCKS], F32, name=name)
@@ -163,24 +177,9 @@ def tile_quantumneuralnetwork_pb_s_kernel(tc, h3, q2_qw, q2_cw, q2_cb, w3, b3, o
 
         yx = product("yx", trig[:, :, PH0, :], twice(trig[:, SIN, TH0, :]))
         z_part = product("z_part", trig[:, :, TH1, :], twice(trig[:, COS, TH0, :]))
-
-        h3_words = h3_rows[:].bitcast(F32)
-        h3_t = psum.tile([P, PASSES, 2, B], F32)
-        for c in range(PASSES):
-            for u in range(2):
-                nc.tensor.transpose(
-                    h3_t[:, c, u, :],
-                    h3_words[:, c * 2 * P + u : (c + 1) * 2 * P : 2],
-                    ident_f32[:],
-                )
-        h3_grouped = keep.tile([P, PASSES, B, 2], F32, align_bytes=64)
-        nc.scalar.copy(out=h3_grouped[:], in_=h3_t[:].rearrange("p c u b -> p c b u"))
-        h3_codes = keep.tile([P, PASSES, B], U32, align_bytes=64)
-        h3_scales = keep.tile([P, PASSES, B], U8, align_bytes=64)
-
-        regroup_chunk(1)
+        quantise_chunk(0, upper)
         x_part = product("x_part", trig[:, :, TH1, :], twice(yx[:, 1, :]))
-        quantise_chunk(0, lower)
+        quantise_chunk(1, lower)
         xz = keep.tile([P, 2, BLOCKS], F32)
         nc.vector.tensor_tensor(
             out=yx[:, 1, :], in0=x_part[:, COS, :], in1=z_part[:, SIN, :], op=ALU.add
@@ -188,29 +187,24 @@ def tile_quantumneuralnetwork_pb_s_kernel(tc, h3, q2_qw, q2_cw, q2_cb, w3, b3, o
         nc.vector.tensor_tensor(
             out=xz[:, 1, :], in0=z_part[:, COS, :], in1=x_part[:, SIN, :], op=ALU.subtract
         )
-        quantise_chunk(0, upper)
+        regroup_chunk(2)
         yx_part = product("yx_part", yx[:], trig[:, :, PH1, :])
-        nc.vector.quantize_mx(
-            out=h3_codes[:].rearrange("p c b -> p (c b)").bitcast(FP8X4),
-            scales=h3_scales[:].rearrange("p c b -> p (c b)"),
-            in_=h3_grouped[:].rearrange("p c b u -> p (c b u)").bitcast(BF16),
-        )
+        quantise_chunk(1, upper)
         nc.vector.tensor_tensor(
             out=xz[:, 0, :], in0=yx_part[:, 1, :], in1=yx_part[:, 0, :], op=ALU.subtract
         )
-        regroup_chunk(2)
+        quantise_chunk(2, lower)
         xz_part = product("xz_part", xz[:], trig[:, :, TH2, :])
-        quantise_chunk(1, lower)
+        regroup_chunk(3)
         z_last = keep.tile([P, BLOCKS], F32)
         nc.vector.tensor_tensor(
             out=z_last[:], in0=xz_part[:, 1, :], in1=xz_part[:, 0, :], op=ALU.subtract
         )
-        quantise_chunk(1, upper)
+        quantise_chunk(2, upper)
         bias = keep.tile([P, BLOCKS], F32)
         nc.vector.scalar_tensor_tensor(
             out=bias[:], in0=z_last[:], scalar=0.5, in1=cb_half[:], op0=ALU.mult, op1=ALU.add
         )
-        regroup_chunk(3)
 
         h4_t = [keep.tile([P, PACK, B], BF16, name="h4_t_%d" % g) for g in range(PASSES)]
 
@@ -234,9 +228,8 @@ def tile_quantumneuralnetwork_pb_s_kernel(tc, h3, q2_qw, q2_cw, q2_cb, w3, b3, o
                 )
 
         first_product(0)
-        for i in range(PASSES, CHUNKS):
-            quantise_chunk(i, lower)
-            quantise_chunk(i, upper)
+        quantise_chunk(3, lower)
+        quantise_chunk(3, upper)
         first_product(1)
 
         w3_grouped = keep.tile([P, PASSES, D_OUT, PACK], BF16, align_bytes=64)

@@ -76,6 +76,9 @@ def tile_quantumneuralnetwork_pb_s_kernel(tc, h3, q2_qw, q2_cw, q2_cb, w3, b3, o
             out=small_rows[0:BLOCKS, K_PASS : K_PASS + P],
             in_=q2_cb.rearrange("(n j) -> n j", j=P),
         )
+        nc.sync.dma_start(
+            out=small_rows[BLOCKS : BLOCKS + 1, K_PASS : K_PASS + P], in_=b3.unsqueeze(0)
+        )
         cw_rows = [
             keep.tile([P, PACK, K_PASS], BF16, name="cw_rows_%d" % i) for i in range(CHUNKS)
         ]
@@ -92,8 +95,6 @@ def tile_quantumneuralnetwork_pb_s_kernel(tc, h3, q2_qw, q2_cw, q2_cb, w3, b3, o
             out=w3_rows[:].rearrange("p g t n -> p (g t) n"),
             in_=w3.rearrange("(s p) n -> p s n", p=P),
         )
-        b3_all = keep.tile([P, D_OUT], BF16)
-        nc.sync.dma_start(out=b3_all[:], in_=b3.partition_broadcast(P))
 
         cw_grouped = [
             keep.tile([P, K_PASS, PACK], BF16, align_bytes=64, name="cw_grouped_%d" % i)
@@ -139,6 +140,13 @@ def tile_quantumneuralnetwork_pb_s_kernel(tc, h3, q2_qw, q2_cw, q2_cb, w3, b3, o
             start=True, stop=True,
         )
         angles = small_t[:, 0:2, :].rearrange("p a r -> p (a r)")
+        b3_row = ident_bf[:, BLOCKS : BLOCKS + 1].to_broadcast([P, P])
+        b3_t = psum.tile([P, D_OUT], F32)
+        nc.tensor.matmul(
+            out=b3_t[:], lhsT=b3_row, rhs=small_rows[:, K_PASS : K_PASS + P], start=True, stop=True
+        )
+        b3_all = keep.tile([P, D_OUT], F32)
+        nc.scalar.copy(out=b3_all[:], in_=b3_t[:])
 
         turns = keep.tile([P, 2, SLOTS * BLOCKS], F32)
         nc.vector.scalar_tensor_tensor(

@@ -25,8 +25,8 @@ RUN = 4
 CHUNKS = PASSES * PASSES
 HALF = K_PASS // 2
 
-TH0, TH1, TH2, PH0, PH1 = 0, 1, 2, 4, 5
-SLOTS = 8
+TH0, TH1, TH2, PH0, PH1 = 0, 1, 2, 3, 4
+SLOTS = 5
 SIN, COS = 0, 1
 
 FLOPS = 2 * B * H * H + 2 * B * H * D_OUT
@@ -76,9 +76,6 @@ def tile_quantumneuralnetwork_pb_s_kernel(tc, h3, q2_qw, q2_cw, q2_cb, w3, b3, o
             out=small_rows[0:BLOCKS, K_PASS : K_PASS + P],
             in_=q2_cb.rearrange("(n j) -> n j", j=P),
         )
-        nc.sync.dma_start(
-            out=small_rows[BLOCKS : BLOCKS + 1, K_PASS : K_PASS + P], in_=b3.unsqueeze(0)
-        )
         cw_rows = [
             keep.tile([P, PACK, K_PASS], BF16, name="cw_rows_%d" % i) for i in range(CHUNKS)
         ]
@@ -95,6 +92,8 @@ def tile_quantumneuralnetwork_pb_s_kernel(tc, h3, q2_qw, q2_cw, q2_cb, w3, b3, o
             out=w3_rows[:].rearrange("p g t n -> p (g t) n"),
             in_=w3.rearrange("(s p) n -> p s n", p=P),
         )
+        b3_all = keep.tile([P, D_OUT], BF16)
+        nc.sync.dma_start(out=b3_all[:], in_=b3.partition_broadcast(P))
 
         cw_grouped = [
             keep.tile([P, K_PASS, PACK], BF16, align_bytes=64, name="cw_grouped_%d" % i)
@@ -130,23 +129,22 @@ def tile_quantumneuralnetwork_pb_s_kernel(tc, h3, q2_qw, q2_cw, q2_cb, w3, b3, o
 
         theta = small_rows[:, 0:K_PASS:4]
         phi = small_rows[:, 3:K_PASS:4]
-        first_rows = ident_bf[:, 0 : 4 * BLOCKS]
-        small_t = psum.tile([P, 3, 4 * BLOCKS], F32)
-        nc.tensor.matmul(out=small_t[:, 0, :], lhsT=theta, rhs=first_rows, start=True, stop=False)
-        nc.tensor.matmul(out=small_t[:, 0, :], lhsT=theta, rhs=first_rows, start=False, stop=True)
-        nc.tensor.matmul(out=small_t[:, 1, :], lhsT=phi, rhs=first_rows, start=True, stop=True)
-        nc.tensor.matmul(
-            out=small_t[:, 2, :], lhsT=small_rows[:, K_PASS : K_PASS + P], rhs=first_rows,
-            start=True, stop=True,
-        )
-        angles = small_t[:, 0:2, :].rearrange("p a r -> p (a r)")
-        b3_row = ident_bf[:, BLOCKS : BLOCKS + 1].to_broadcast([P, P])
-        b3_t = psum.tile([P, D_OUT], F32)
-        nc.tensor.matmul(
-            out=b3_t[:], lhsT=b3_row, rhs=small_rows[:, K_PASS : K_PASS + P], start=True, stop=True
-        )
-        b3_all = keep.tile([P, D_OUT], F32)
-        nc.scalar.copy(out=b3_all[:], in_=b3_t[:])
+        small_t = psum.tile([P, SLOTS + 1, BLOCKS], F32)
+
+        def rows_to_columns(first_slot, slots, rows, start=True, stop=True):
+            nc.tensor.matmul(
+                out=small_t[:, first_slot : first_slot + slots, :].rearrange("p a n -> p (a n)"),
+                lhsT=rows,
+                rhs=ident_bf[:, 0 : slots * BLOCKS],
+                start=start,
+                stop=stop,
+            )
+
+        rows_to_columns(TH0, 3, theta, stop=False)
+        rows_to_columns(TH0, 3, theta, start=False)
+        rows_to_columns(PH0, 2, phi)
+        rows_to_columns(SLOTS, 1, small_rows[:, K_PASS : K_PASS + P])
+        angles = small_t[:, 0:SLOTS, :].rearrange("p a n -> p (a n)")
 
         turns = keep.tile([P, 2, SLOTS * BLOCKS], F32)
         nc.vector.scalar_tensor_tensor(
@@ -159,7 +157,7 @@ def tile_quantumneuralnetwork_pb_s_kernel(tc, h3, q2_qw, q2_cw, q2_cb, w3, b3, o
         )
         cb_half = keep.tile([P, BLOCKS], F32)
         nc.vector.tensor_scalar(
-            out=cb_half[:], in0=small_t[:, 2, 0:BLOCKS], scalar1=0.5, scalar2=None, op0=ALU.add
+            out=cb_half[:], in0=small_t[:, SLOTS, :], scalar1=0.5, scalar2=None, op0=ALU.add
         )
         regroup_chunk(0)
         whole = keep.tile([P, 2, SLOTS * BLOCKS], I32)
@@ -176,7 +174,6 @@ def tile_quantumneuralnetwork_pb_s_kernel(tc, h3, q2_qw, q2_cw, q2_cb, w3, b3, o
             scale=2.0 * math.pi,
         )
         quantise_chunk(0, lower)
-        regroup_chunk(1)
 
         def product(name, in0, in1):
             pair = keep.tile([P, 2, BLOCKS], F32, name=name)
@@ -185,9 +182,9 @@ def tile_quantumneuralnetwork_pb_s_kernel(tc, h3, q2_qw, q2_cw, q2_cb, w3, b3, o
 
         yx = product("yx", trig[:, :, PH0, :], twice(trig[:, SIN, TH0, :]))
         z_part = product("z_part", trig[:, :, TH1, :], twice(trig[:, COS, TH0, :]))
-        quantise_chunk(0, upper)
+        regroup_chunk(1)
         x_part = product("x_part", trig[:, :, TH1, :], twice(yx[:, 1, :]))
-        quantise_chunk(1, lower)
+        quantise_chunk(0, upper)
         xz = keep.tile([P, 2, BLOCKS], F32)
         nc.vector.tensor_tensor(
             out=yx[:, 1, :], in0=x_part[:, COS, :], in1=z_part[:, SIN, :], op=ALU.add
@@ -195,24 +192,25 @@ def tile_quantumneuralnetwork_pb_s_kernel(tc, h3, q2_qw, q2_cw, q2_cb, w3, b3, o
         nc.vector.tensor_tensor(
             out=xz[:, 1, :], in0=z_part[:, COS, :], in1=x_part[:, SIN, :], op=ALU.subtract
         )
-        regroup_chunk(2)
+        quantise_chunk(1, lower)
         yx_part = product("yx_part", yx[:], trig[:, :, PH1, :])
-        quantise_chunk(1, upper)
+        regroup_chunk(2)
         nc.vector.tensor_tensor(
             out=xz[:, 0, :], in0=yx_part[:, 1, :], in1=yx_part[:, 0, :], op=ALU.subtract
         )
-        quantise_chunk(2, lower)
+        quantise_chunk(1, upper)
         xz_part = product("xz_part", xz[:], trig[:, :, TH2, :])
-        regroup_chunk(3)
+        quantise_chunk(2, lower)
         z_last = keep.tile([P, BLOCKS], F32)
         nc.vector.tensor_tensor(
             out=z_last[:], in0=xz_part[:, 1, :], in1=xz_part[:, 0, :], op=ALU.subtract
         )
-        quantise_chunk(2, upper)
+        regroup_chunk(3)
         bias = keep.tile([P, BLOCKS], F32)
         nc.vector.scalar_tensor_tensor(
             out=bias[:], in0=z_last[:], scalar=0.5, in1=cb_half[:], op0=ALU.mult, op1=ALU.add
         )
+        quantise_chunk(2, upper)
 
         h4_t = [keep.tile([P, PACK, B], BF16, name="h4_t_%d" % g) for g in range(PASSES)]
 

@@ -25,9 +25,9 @@ RUN = 4
 CHUNKS = PASSES * PASSES
 HALF = K_PASS // 2
 
-TH0, TH1, TH2, PH0, PH1 = 0, 1, 2, 3, 4
+PH0, PH1, TH0, TH1, TH2 = 0, 1, 2, 3, 4
 SLOTS = 5
-SIN, COS = 0, 1
+NSIN, COS, SIN = 0, 1, 2
 
 FLOPS = 2 * B * H * H + 2 * B * H * D_OUT
 
@@ -48,38 +48,28 @@ def tile_quantumneuralnetwork_pb_s_kernel(tc, h3, q2_qw, q2_cw, q2_cb, w3, b3, o
     lower, upper = slice(0, HALF), slice(HALF, K_PASS)
     with ExitStack() as ctx:
         keep = ctx.enter_context(tc.tile_pool(name="keep", bufs=1))
-        psum = ctx.enter_context(tc.psum_pool(name="psum", bufs=1))
-        acc_pool = ctx.enter_context(tc.psum_pool(name="acc_pool", bufs=UNITS))
+        psum = ctx.enter_context(tc.psum_pool(name="psum", bufs=8))
         ctx.enter_context(tc.manual_schedule())
 
-        small_rows = keep.tile([P, K_PASS + P], BF16)
+        small_rows = keep.tile([P, DEPTH * K_PASS + P], BF16)
         nc.gpsimd.memset(small_rows[:].bitcast(F32), 0.0)
         ident_f32 = keep.tile([P, P], F32)
         make_identity(nc, ident_f32[:])
         ident_bf = keep.tile([P, P], BF16)
         make_identity(nc, ident_bf[:])
-        phase = keep.tile([P, 2, SLOTS * BLOCKS], F32)
-        nc.vector.memset(phase[:, SIN, :], 0.0)
+        phase = keep.tile([P, 3, SLOTS * BLOCKS], F32)
+        nc.vector.memset(phase[:, NSIN, :], 0.5)
         nc.vector.memset(phase[:, COS, :], 0.25)
+        nc.vector.memset(phase[:, SIN, :], 0.0)
         warm = keep.tile([P, 1], F32)
         nc.vector.memset(warm[:], 0.0)
         nc.scalar.activation(out=warm[:], in_=warm[:], func=ACT.Silu)
 
-        h3_rows = keep.tile([P, H], BF16)
-        nc.sync.dma_start(out=h3_rows[:], in_=h3)
-        for d in range(DEPTH):
-            nc.sync.dma_start(
-                out=small_rows[d * BLOCKS : (d + 1) * BLOCKS, 0:K_PASS],
-                in_=q2_qw[d].rearrange("(n j) a b -> n (j a b)", j=P),
-            )
-        nc.sync.dma_start(
-            out=small_rows[0:BLOCKS, K_PASS : K_PASS + P],
-            in_=q2_cb.rearrange("(n j) -> n j", j=P),
-        )
         cw_rows = [
             keep.tile([P, PACK, K_PASS], BF16, name="cw_rows_%d" % i) for i in range(CHUNKS)
         ]
-        for i in range(CHUNKS):
+
+        def load_chunk(i):
             g, c = divmod(i, PASSES)
             nc.sync.dma_start(
                 out=cw_rows[i][:],
@@ -87,6 +77,21 @@ def tile_quantumneuralnetwork_pb_s_kernel(tc, h3, q2_qw, q2_cw, q2_cb, w3, b3, o
                     c * K_PASS : (c + 1) * K_PASS, g * K_PASS : (g + 1) * K_PASS
                 ].rearrange("(p t) w -> p t w", t=PACK),
             )
+
+        load_chunk(0)
+        nc.sync.dma_start(
+            out=small_rows[0:BLOCKS, 0 : DEPTH * K_PASS].rearrange("n (d w) -> n d w", d=DEPTH),
+            in_=q2_qw.rearrange("d (n j) a b -> n d (j a b)", j=P),
+        )
+        nc.sync.dma_start(
+            out=small_rows[0:BLOCKS, DEPTH * K_PASS : DEPTH * K_PASS + P],
+            in_=q2_cb.rearrange("(n j) -> n j", j=P),
+        )
+        load_chunk(1)
+        h3_rows = keep.tile([P, H], BF16)
+        nc.sync.dma_start(out=h3_rows[:], in_=h3)
+        load_chunk(2)
+        load_chunk(3)
         w3_rows = keep.tile([P, PASSES, PACK, D_OUT], BF16)
         nc.sync.dma_start(
             out=w3_rows[:].rearrange("p g t n -> p (g t) n"),
@@ -113,8 +118,56 @@ def tile_quantumneuralnetwork_pb_s_kernel(tc, h3, q2_qw, q2_cw, q2_cb, w3, b3, o
                 in_=cw_grouped[i][:, half, :].rearrange("p w t -> p (w t)"),
             )
 
+        small_t = psum.tile([P, SLOTS + 1, BLOCKS], F32, tag="bank")
+
+        def rows_to_column(slot, rows, start=True, stop=True):
+            nc.tensor.matmul(
+                out=small_t[:, slot, :], lhsT=rows, rhs=ident_bf[:, 0:BLOCKS],
+                start=start, stop=stop,
+            )
+
+        def entry(d, i):
+            return small_rows[:, d * K_PASS + i : (d + 1) * K_PASS : 4]
+
+        for d in range(DEPTH):
+            rows_to_column(TH0 + d, entry(d, 0), stop=False)
+            rows_to_column(TH0 + d, entry(d, 0), start=False)
+        for d in range(DEPTH - 1):
+            rows_to_column(PH0 + d, entry(d, 3))
+        rows_to_column(SLOTS, small_rows[:, DEPTH * K_PASS : DEPTH * K_PASS + P])
+        angles = small_t[:, 0:SLOTS, :].rearrange("p a n -> p (a n)")
+
+        regroup_chunk(0)
+        turns = keep.tile([P, 3, SLOTS * BLOCKS], F32)
+        nc.vector.scalar_tensor_tensor(
+            out=turns[:],
+            in0=angles.unsqueeze(1).to_broadcast([P, 3, SLOTS * BLOCKS]),
+            scalar=1.0 / (2.0 * math.pi),
+            in1=phase[:],
+            op0=ALU.mult,
+            op1=ALU.add,
+        )
+        terms = keep.tile([P, 4, BLOCKS], F32)
+        nc.vector.tensor_scalar(
+            out=terms[:, 3, :], in0=small_t[:, SLOTS, :], scalar1=0.5, scalar2=None, op0=ALU.add
+        )
+        quantise_chunk(0, lower)
+        whole = keep.tile([P, 3, SLOTS * BLOCKS], I32)
+        nc.vector.tensor_copy(out=whole[:], in_=turns[:])
+        quantise_chunk(0, upper)
+        nc.vector.tensor_tensor(out=turns[:], in0=turns[:], in1=whole[:], op=ALU.subtract)
+        regroup_chunk(1)
+        trig = keep.tile([P, 3, SLOTS + 2, BLOCKS], F32)
+        nc.scalar.activation(
+            out=trig[:, :, 0:SLOTS, :].rearrange("p f a n -> p f (a n)"),
+            in_=turns[:],
+            func=ACT.Sin,
+            scale=2.0 * math.pi,
+        )
+        quantise_chunk(1, lower)
+
         h3_words = h3_rows[:].bitcast(F32)
-        h3_t = psum.tile([P, PASSES, 2, B], F32)
+        h3_t = psum.tile([P, PASSES, 2, B], F32, tag="bank")
         for c in range(PASSES):
             for u in range(2):
                 nc.tensor.transpose(
@@ -127,116 +180,77 @@ def tile_quantumneuralnetwork_pb_s_kernel(tc, h3, q2_qw, q2_cw, q2_cb, w3, b3, o
         h3_codes = keep.tile([P, PASSES, B], U32, align_bytes=64)
         h3_scales = keep.tile([P, PASSES, B], U8, align_bytes=64)
 
-        theta = small_rows[:, 0:K_PASS:4]
-        phi = small_rows[:, 3:K_PASS:4]
-        small_t = psum.tile([P, SLOTS + 1, BLOCKS], F32)
-
-        def rows_to_columns(first_slot, slots, rows, start=True, stop=True):
-            nc.tensor.matmul(
-                out=small_t[:, first_slot : first_slot + slots, :].rearrange("p a n -> p (a n)"),
-                lhsT=rows,
-                rhs=ident_bf[:, 0 : slots * BLOCKS],
-                start=start,
-                stop=stop,
-            )
-
-        rows_to_columns(TH0, 3, theta, stop=False)
-        rows_to_columns(TH0, 3, theta, start=False)
-        rows_to_columns(PH0, 2, phi)
-        rows_to_columns(SLOTS, 1, small_rows[:, K_PASS : K_PASS + P])
-        angles = small_t[:, 0:SLOTS, :].rearrange("p a n -> p (a n)")
-
-        turns = keep.tile([P, 2, SLOTS * BLOCKS], F32)
+        quantise_chunk(1, upper)
+        zxy = keep.tile([P, 3, BLOCKS], F32)
         nc.vector.scalar_tensor_tensor(
-            out=turns[:],
-            in0=angles.unsqueeze(1).to_broadcast([P, 2, SLOTS * BLOCKS]),
-            scalar=1.0 / (2.0 * math.pi),
-            in1=phase[:],
-            op0=ALU.mult,
-            op1=ALU.add,
+            out=zxy[:, 1:3, :], in0=trig[:, COS : SIN + 1, PH0, :], scalar=0.5,
+            in1=twice(trig[:, SIN, TH0, :]), op0=ALU.mult, op1=ALU.mult,
         )
-        cb_half = keep.tile([P, BLOCKS], F32)
-        nc.vector.tensor_scalar(
-            out=cb_half[:], in0=small_t[:, SLOTS, :], scalar1=0.5, scalar2=None, op0=ALU.add
+        from_z = keep.tile([P, 2, BLOCKS], F32)
+        nc.vector.scalar_tensor_tensor(
+            out=from_z[:], in0=trig[:, COS : SIN + 1, TH1, :], scalar=0.5,
+            in1=twice(trig[:, COS, TH0, :]), op0=ALU.mult, op1=ALU.mult,
         )
-        regroup_chunk(0)
-        whole = keep.tile([P, 2, SLOTS * BLOCKS], I32)
-        nc.vector.tensor_copy(out=whole[:], in_=turns[:])
+        nc.vector.tensor_tensor(
+            out=trig[:, COS, SLOTS : SLOTS + 2, :], in0=trig[:, COS::-1, PH1, :],
+            in1=twice(trig[:, NSIN, TH2, :]), op=ALU.mult,
+        )
+        regroup_chunk(2)
+        from_x = keep.tile([P, 2, BLOCKS], F32)
+        nc.vector.tensor_tensor(
+            out=from_x[:], in0=trig[:, NSIN : COS + 1, TH1, :], in1=twice(zxy[:, 1, :]),
+            op=ALU.mult,
+        )
         nc.vector.quantize_mx(
             out=h3_codes[:].rearrange("p c b -> p (c b)").bitcast(FP8X4),
             scales=h3_scales[:].rearrange("p c b -> p (c b)"),
             in_=h3_grouped[:].rearrange("p c b u -> p (c b u)").bitcast(BF16),
         )
-        nc.vector.tensor_tensor(out=turns[:], in0=turns[:], in1=whole[:], op=ALU.subtract)
-        trig = keep.tile([P, 2, SLOTS, BLOCKS], F32)
-        nc.scalar.activation(
-            out=trig[:].rearrange("p f a n -> p f (a n)"), in_=turns[:], func=ACT.Sin,
-            scale=2.0 * math.pi,
-        )
-        quantise_chunk(0, lower)
-
-        def product(name, in0, in1):
-            pair = keep.tile([P, 2, BLOCKS], F32, name=name)
-            nc.vector.tensor_tensor(out=pair[:], in0=in0, in1=in1, op=ALU.mult)
-            return pair
-
-        yx = product("yx", trig[:, :, PH0, :], twice(trig[:, SIN, TH0, :]))
-        z_part = product("z_part", trig[:, :, TH1, :], twice(trig[:, COS, TH0, :]))
-        regroup_chunk(1)
-        x_part = product("x_part", trig[:, :, TH1, :], twice(yx[:, 1, :]))
-        quantise_chunk(0, upper)
-        xz = keep.tile([P, 2, BLOCKS], F32)
-        nc.vector.tensor_tensor(
-            out=yx[:, 1, :], in0=x_part[:, COS, :], in1=z_part[:, SIN, :], op=ALU.add
-        )
-        nc.vector.tensor_tensor(
-            out=xz[:, 1, :], in0=z_part[:, COS, :], in1=x_part[:, SIN, :], op=ALU.subtract
-        )
-        quantise_chunk(1, lower)
-        yx_part = product("yx_part", yx[:], trig[:, :, PH1, :])
-        regroup_chunk(2)
-        nc.vector.tensor_tensor(
-            out=xz[:, 0, :], in0=yx_part[:, 1, :], in1=yx_part[:, 0, :], op=ALU.subtract
-        )
-        quantise_chunk(1, upper)
-        xz_part = product("xz_part", xz[:], trig[:, :, TH2, :])
+        nc.vector.tensor_tensor(out=zxy[:, 0:2, :], in0=from_z[:], in1=from_x[:], op=ALU.add)
         quantise_chunk(2, lower)
-        z_last = keep.tile([P, BLOCKS], F32)
         nc.vector.tensor_tensor(
-            out=z_last[:], in0=xz_part[:, 1, :], in1=xz_part[:, 0, :], op=ALU.subtract
+            out=terms[:, 0:3, :], in0=trig[:, COS, TH2 : TH2 + 3, :], in1=zxy[:], op=ALU.mult
         )
         regroup_chunk(3)
         bias = keep.tile([P, BLOCKS], F32)
-        nc.vector.scalar_tensor_tensor(
-            out=bias[:], in0=z_last[:], scalar=0.5, in1=cb_half[:], op0=ALU.mult, op1=ALU.add
+        nc.vector.tensor_reduce(
+            out=bias[:], in_=terms[:].rearrange("p r n -> p n r"), op=ALU.add,
+            axis=mybir.AxisListType.X,
         )
         quantise_chunk(2, upper)
 
         h4_t = [keep.tile([P, PACK, B], BF16, name="h4_t_%d" % g) for g in range(PASSES)]
 
-        def first_product(g):
+        acc = [psum.tile([P, B], F32, tag="bank", name="acc_%d" % n) for n in range(BLOCKS)]
+
+        def first_product(g, c):
             for t in range(UNITS):
                 units = slice(t * P, (t + 1) * P)
-                acc = acc_pool.tile([P, B], F32)
-                for c in range(PASSES):
-                    nc.tensor.matmul_mx(
-                        out=acc[:],
-                        lhsT=cw_codes[:, g * PASSES + c, units].bitcast(FP8X4),
-                        lhsT_scale=cw_scales[:, g * PASSES + c, units],
-                        rhs=h3_codes[:, c, :].bitcast(FP8X4),
-                        rhs_scale=h3_scales[:, c, :],
-                        start=(c == 0),
-                        stop=(c == PASSES - 1),
-                    )
-                n = g * UNITS + t
-                nc.scalar.activation(
-                    out=h4_t[g][:, t, :], in_=acc[:], func=ACT.Tanh, bias=bias[:, n : n + 1]
+                nc.tensor.matmul_mx(
+                    out=acc[g * UNITS + t][:],
+                    lhsT=cw_codes[:, g * PASSES + c, units].bitcast(FP8X4),
+                    lhsT_scale=cw_scales[:, g * PASSES + c, units],
+                    rhs=h3_codes[:, c, :].bitcast(FP8X4),
+                    rhs_scale=h3_scales[:, c, :],
+                    start=(c == 0),
+                    stop=(c == PASSES - 1),
                 )
 
-        first_product(0)
+        def tanh(g):
+            for t in range(UNITS):
+                n = g * UNITS + t
+                nc.scalar.activation(
+                    out=h4_t[g][:, t, :], in_=acc[n][:], func=ACT.Tanh, bias=bias[:, n : n + 1]
+                )
+
+        first_product(0, 0)
+        first_product(0, 1)
+        tanh(0)
+        first_product(1, 0)
         quantise_chunk(3, lower)
         quantise_chunk(3, upper)
-        first_product(1)
+        first_product(1, 1)
+        tanh(1)
 
         w3_grouped = keep.tile([P, PASSES, D_OUT, PACK], BF16, align_bytes=64)
         w3_codes = keep.tile([P, PASSES, D_OUT], U32, align_bytes=64)
@@ -244,7 +258,7 @@ def tile_quantumneuralnetwork_pb_s_kernel(tc, h3, q2_qw, q2_cw, q2_cb, w3, b3, o
         h4_grouped = keep.tile([P, PASSES, B, PACK], BF16, align_bytes=64)
         h4_codes = keep.tile([P, PASSES, B], U32, align_bytes=64)
         h4_scales = keep.tile([P, PASSES, B], U8, align_bytes=64)
-        out_acc = psum.tile([B, D_OUT], F32)
+        out_acc = psum.tile([B, D_OUT], F32, tag="bank")
 
         def quantise_h4(g):
             nc.vector.quantize_mx(

@@ -24,6 +24,7 @@ RUN = 4
 
 CHUNKS = PASSES * PASSES
 HALF = K_PASS // 2
+VECTOR_SHARE = 272
 
 PH0, PH1, TH0, TH1, TH2 = 0, 1, 2, 3, 4
 SLOTS = 5
@@ -57,10 +58,9 @@ def tile_quantumneuralnetwork_pb_s_kernel(tc, h3, q2_qw, q2_cw, q2_cb, w3, b3, o
         make_identity(nc, ident_f32[:])
         ident_bf = keep.tile([P, P], BF16)
         make_identity(nc, ident_bf[:])
-        phase = keep.tile([P, 3, SLOTS * BLOCKS], F32)
-        nc.vector.memset(phase[:, NSIN, :], 0.5)
-        nc.vector.memset(phase[:, COS, :], 0.25)
-        nc.vector.memset(phase[:, SIN, :], 0.0)
+        phase = keep.tile([P, 2, SLOTS * BLOCKS], F32)
+        nc.vector.memset(phase[:, 0, :], 0.0)
+        nc.vector.memset(phase[:, 1, :], 0.25)
         warm = keep.tile([P, 1], F32)
         nc.vector.memset(warm[:], 0.0)
         nc.scalar.activation(out=warm[:], in_=warm[:], func=ACT.Silu)
@@ -108,8 +108,9 @@ def tile_quantumneuralnetwork_pb_s_kernel(tc, h3, q2_qw, q2_cw, q2_cb, w3, b3, o
         cw_scales = keep.tile([P, CHUNKS, K_PASS], U8, align_bytes=64)
 
         def regroup_chunk(i):
-            regroup(nc.vector.tensor_copy, cw_grouped[i][:, lower, :], cw_rows[i][:, :, lower])
-            regroup(nc.scalar.copy, cw_grouped[i][:, upper, :], cw_rows[i][:, :, upper])
+            first, rest = slice(0, VECTOR_SHARE), slice(VECTOR_SHARE, K_PASS)
+            regroup(nc.vector.tensor_copy, cw_grouped[i][:, first, :], cw_rows[i][:, :, first])
+            regroup(nc.scalar.copy, cw_grouped[i][:, rest, :], cw_rows[i][:, :, rest])
 
         def quantise_chunk(i, half):
             nc.vector.quantize_mx(
@@ -138,34 +139,33 @@ def tile_quantumneuralnetwork_pb_s_kernel(tc, h3, q2_qw, q2_cw, q2_cb, w3, b3, o
         angles = small_t[:, 0:SLOTS, :].rearrange("p a n -> p (a n)")
 
         regroup_chunk(0)
-        turns = keep.tile([P, 3, SLOTS * BLOCKS], F32)
+        whole = keep.tile([P, 2, SLOTS * BLOCKS], I32)
         nc.vector.scalar_tensor_tensor(
-            out=turns[:],
-            in0=angles.unsqueeze(1).to_broadcast([P, 3, SLOTS * BLOCKS]),
-            scalar=1.0 / (2.0 * math.pi),
-            in1=phase[:],
-            op0=ALU.mult,
-            op1=ALU.add,
-        )
-        terms = keep.tile([P, 4, BLOCKS], F32)
-        nc.vector.tensor_scalar(
-            out=terms[:, 3, :], in0=small_t[:, SLOTS, :], scalar1=0.5, scalar2=None, op0=ALU.add
+            out=whole[:], in0=angles.unsqueeze(1).to_broadcast([P, 2, SLOTS * BLOCKS]),
+            scalar=1.0 / (2.0 * math.pi), in1=phase[:], op0=ALU.mult, op1=ALU.add,
         )
         quantise_chunk(0, lower)
-        whole = keep.tile([P, 3, SLOTS * BLOCKS], I32)
-        nc.vector.tensor_copy(out=whole[:], in_=turns[:])
+        turns = keep.tile([P, 2, SLOTS * BLOCKS], F32)
+        nc.vector.scalar_tensor_tensor(
+            out=turns[:], in0=angles.unsqueeze(1).to_broadcast([P, 2, SLOTS * BLOCKS]),
+            scalar=1.0 / (2.0 * math.pi), in1=whole[:], op0=ALU.mult, op1=ALU.subtract,
+        )
         quantise_chunk(0, upper)
-        nc.vector.tensor_tensor(out=turns[:], in0=turns[:], in1=whole[:], op=ALU.subtract)
         regroup_chunk(1)
         trig = keep.tile([P, 3, SLOTS + 2, BLOCKS], F32)
+        for row, source, scale, bias_angle in (
+            (SIN, 0, 2.0 * math.pi, 0.0),
+            (COS, 1, 2.0 * math.pi, 0.5 * math.pi),
+            (NSIN, 0, -2.0 * math.pi, 0.0),
+        ):
+            nc.scalar.activation(
+                out=trig[:, row, 0:SLOTS, :].rearrange("p a n -> p (a n)"),
+                in_=turns[:, source, :], func=ACT.Sin, scale=scale, bias=bias_angle,
+            )
+        terms = keep.tile([P, 4, BLOCKS], F32)
         nc.scalar.activation(
-            out=trig[:, :, 0:SLOTS, :].rearrange("p f a n -> p f (a n)"),
-            in_=turns[:],
-            func=ACT.Sin,
-            scale=2.0 * math.pi,
+            out=terms[:, 3, :], in_=small_t[:, SLOTS, :], func=ACT.Identity, bias=0.5
         )
-        quantise_chunk(1, lower)
-
         h3_words = h3_rows[:].bitcast(F32)
         h3_t = psum.tile([P, PASSES, 2, B], F32, tag="bank")
         for c in range(PASSES):
@@ -180,6 +180,7 @@ def tile_quantumneuralnetwork_pb_s_kernel(tc, h3, q2_qw, q2_cw, q2_cb, w3, b3, o
         h3_codes = keep.tile([P, PASSES, B], U32, align_bytes=64)
         h3_scales = keep.tile([P, PASSES, B], U8, align_bytes=64)
 
+        quantise_chunk(1, lower)
         quantise_chunk(1, upper)
         zxy = keep.tile([P, 3, BLOCKS], F32)
         nc.vector.scalar_tensor_tensor(
@@ -208,16 +209,16 @@ def tile_quantumneuralnetwork_pb_s_kernel(tc, h3, q2_qw, q2_cw, q2_cb, w3, b3, o
         )
         nc.vector.tensor_tensor(out=zxy[:, 0:2, :], in0=from_z[:], in1=from_x[:], op=ALU.add)
         quantise_chunk(2, lower)
+        regroup_chunk(3)
         nc.vector.tensor_tensor(
             out=terms[:, 0:3, :], in0=trig[:, COS, TH2 : TH2 + 3, :], in1=zxy[:], op=ALU.mult
         )
-        regroup_chunk(3)
+        quantise_chunk(2, upper)
         bias = keep.tile([P, BLOCKS], F32)
         nc.vector.tensor_reduce(
             out=bias[:], in_=terms[:].rearrange("p r n -> p n r"), op=ALU.add,
             axis=mybir.AxisListType.X,
         )
-        quantise_chunk(2, upper)
 
         h4_t = [keep.tile([P, PACK, B], BF16, name="h4_t_%d" % g) for g in range(PASSES)]
 
@@ -286,15 +287,20 @@ def tile_quantumneuralnetwork_pb_s_kernel(tc, h3, q2_qw, q2_cw, q2_cb, w3, b3, o
             scales=w3_scales[:].rearrange("p g n -> p (g n)"),
             in_=w3_grouped[:].rearrange("p g n t -> p (g n t)"),
         )
+        regroup(nc.vector.tensor_copy, h4_grouped[:, 1, :, :], h4_t[1][:])
         quantise_h4(0)
         second_product(0)
-        regroup(nc.vector.tensor_copy, h4_grouped[:, 1, :, :], h4_t[1][:])
         quantise_h4(1)
         second_product(1)
 
         result = keep.tile([B, D_OUT], F32)
-        nc.vector.tensor_tensor(out=result[:], in0=out_acc[:], in1=b3_all[:], op=ALU.add)
-        nc.vector.tensor_scalar(
-            out=result[:], in0=result[:], scalar1=0.0, scalar2=None, op0=ALU.max
-        )
+        halves = (slice(0, D_OUT // 2), slice(D_OUT // 2, D_OUT))
+        for half in halves:
+            nc.vector.tensor_tensor(
+                out=result[:, half], in0=out_acc[:, half], in1=b3_all[:, half], op=ALU.add
+            )
+        for half in halves:
+            nc.vector.tensor_scalar(
+                out=result[:, half], in0=result[:, half], scalar1=0.0, scalar2=None, op0=ALU.max
+            )
         nc.sync.dma_start(out=out, in_=result[:])

import math
from contextlib import ExitStack

import concourse.mybir as mybir
from concourse.masks import make_identity

F32 = mybir.dt.float32
BF16 = mybir.dt.bfloat16
I32 = mybir.dt.int32
U32 = mybir.dt.uint32
U8 = mybir.dt.uint8
FP8X4 = mybir.dt.float8_e4m3fn_x4
ACT = mybir.ActivationFunctionType
ALU = mybir.AluOpType

P = 128
PACK = 4
K_PASS = P * PACK
B, H, D_OUT, DEPTH = 128, 1024, 128, 3
PASSES = H // K_PASS
UNITS = K_PASS // P
BLOCKS = H // P
RUN = 4

CHUNKS = PASSES * PASSES
HALF = K_PASS // 2
VECTOR_SHARE = 272

PH0, PH1, TH0, TH1, TH2 = 0, 1, 2, 3, 4
SLOTS = 5
NSIN, COS, SIN = 0, 1, 2

FLOPS = 2 * B * H * H + 2 * B * H * D_OUT


def regroup(copy, grouped, rows):
    copy(
        out=grouped.rearrange("p (c i) t -> p c t i", i=RUN),
        in_=rows.rearrange("p t (c i) -> p c t i", i=RUN),
    )


def twice(column):
    return column.unsqueeze(1).to_broadcast([P, 2, BLOCKS])


def tile_quantumneuralnetwork_pb_s_kernel(tc, h3, q2_qw, q2_cw, q2_cb, w3, b3, out):
    nc = tc.nc
    lower, upper = slice(0, HALF), slice(HALF, K_PASS)
    with ExitStack() as ctx:
        keep = ctx.enter_context(tc.tile_pool(name="keep", bufs=1))
        psum = ctx.enter_context(tc.psum_pool(name="psum", bufs=8))
        ctx.enter_context(tc.manual_schedule())

        small_rows = keep.tile([P, DEPTH * K_PASS + P], BF16)
        nc.gpsimd.memset(small_rows[:].bitcast(F32), 0.0)
        ident_f32 = keep.tile([P, P], F32)
        make_identity(nc, ident_f32[:])
        ident_bf = keep.tile([P, P], BF16)
        make_identity(nc, ident_bf[:])
        phase = keep.tile([P, 2, SLOTS * BLOCKS], F32)
        nc.vector.memset(phase[:, 0, :], 0.0)
        nc.vector.memset(phase[:, 1, :], 0.25)
        warm = keep.tile([P, 1], F32)
        nc.vector.memset(warm[:], 0.0)
        nc.scalar.activation(out=warm[:], in_=warm[:], func=ACT.Silu)

        cw_rows = [
            keep.tile([P, PACK, K_PASS], BF16, name="cw_rows_%d" % i) for i in range(CHUNKS)
        ]

        def load_chunk(i):
            g, c = divmod(i, PASSES)
            nc.sync.dma_start(
                out=cw_rows[i][:],
                in_=q2_cw[
                    c * K_PASS : (c + 1) * K_PASS, g * K_PASS : (g + 1) * K_PASS
                ].rearrange("(p t) w -> p t w", t=PACK),
            )

        load_chunk(0)
        nc.sync.dma_start(
            out=small_rows[0:BLOCKS, 0 : DEPTH * K_PASS].rearrange("n (d w) -> n d w", d=DEPTH),
            in_=q2_qw.rearrange("d (n j) a b -> n d (j a b)", j=P),
        )
        nc.sync.dma_start(
            out=small_rows[0:BLOCKS, DEPTH * K_PASS : DEPTH * K_PASS + P],
            in_=q2_cb.rearrange("(n j) -> n j", j=P),
        )
        load_chunk(1)
        h3_rows = keep.tile([P, H], BF16)
        nc.sync.dma_start(out=h3_rows[:], in_=h3)
        load_chunk(2)
        load_chunk(3)
        w3_rows = keep.tile([P, PASSES, PACK, D_OUT], BF16)
        nc.sync.dma_start(
            out=w3_rows[:].rearrange("p g t n -> p (g t) n"),
            in_=w3.rearrange("(s p) n -> p s n", p=P),
        )
        b3_all = keep.tile([P, D_OUT], BF16)
        nc.sync.dma_start(out=b3_all[:], in_=b3.partition_broadcast(P))

        cw_grouped = [
            keep.tile([P, K_PASS, PACK], BF16, align_bytes=64, name="cw_grouped_%d" % i)
            for i in range(CHUNKS)
        ]
        cw_codes = keep.tile([P, CHUNKS, K_PASS], U32, align_bytes=64)
        cw_scales = keep.tile([P, CHUNKS, K_PASS], U8, align_bytes=64)

        def regroup_chunk(i):
            first, rest = slice(0, VECTOR_SHARE), slice(VECTOR_SHARE, K_PASS)
            regroup(nc.vector.tensor_copy, cw_grouped[i][:, first, :], cw_rows[i][:, :, first])
            regroup(nc.scalar.copy, cw_grouped[i][:, rest, :], cw_rows[i][:, :, rest])

        def quantise_chunk(i, half):
            nc.vector.quantize_mx(
                out=cw_codes[:, i, half].bitcast(FP8X4),
                scales=cw_scales[:, i, half],
                in_=cw_grouped[i][:, half, :].rearrange("p w t -> p (w t)"),
            )

        small_t = psum.tile([P, SLOTS + 1, BLOCKS], F32, tag="bank")

        def rows_to_column(slot, rows, start=True, stop=True):
            nc.tensor.matmul(
                out=small_t[:, slot, :], lhsT=rows, rhs=ident_bf[:, 0:BLOCKS],
                start=start, stop=stop,
            )

        def entry(d, i):
            return small_rows[:, d * K_PASS + i : (d + 1) * K_PASS : 4]

        for d in range(DEPTH):
            rows_to_column(TH0 + d, entry(d, 0), stop=False)
            rows_to_column(TH0 + d, entry(d, 0), start=False)
        for d in range(DEPTH - 1):
            rows_to_column(PH0 + d, entry(d, 3))
        rows_to_column(SLOTS, small_rows[:, DEPTH * K_PASS : DEPTH * K_PASS + P])
        angles = small_t[:, 0:SLOTS, :].rearrange("p a n -> p (a n)")

        regroup_chunk(0)
        whole = keep.tile([P, 2, SLOTS * BLOCKS], I32)
        nc.vector.scalar_tensor_tensor(
            out=whole[:], in0=angles.unsqueeze(1).to_broadcast([P, 2, SLOTS * BLOCKS]),
            scalar=1.0 / (2.0 * math.pi), in1=phase[:], op0=ALU.mult, op1=ALU.add,
        )
        quantise_chunk(0, lower)
        turns = keep.tile([P, 2, SLOTS * BLOCKS], F32)
        nc.vector.scalar_tensor_tensor(
            out=turns[:], in0=angles.unsqueeze(1).to_broadcast([P, 2, SLOTS * BLOCKS]),
            scalar=1.0 / (2.0 * math.pi), in1=whole[:], op0=ALU.mult, op1=ALU.subtract,
        )
        quantise_chunk(0, upper)
        regroup_chunk(1)
        trig = keep.tile([P, 3, SLOTS + 2, BLOCKS], F32)
        for row, source, scale, bias_angle in (
            (SIN, 0, 2.0 * math.pi, 0.0),
            (COS, 1, 2.0 * math.pi, 0.5 * math.pi),
            (NSIN, 0, -2.0 * math.pi, 0.0),
        ):
            nc.scalar.activation(
                out=trig[:, row, 0:SLOTS, :].rearrange("p a n -> p (a n)"),
                in_=turns[:, source, :], func=ACT.Sin, scale=scale, bias=bias_angle,
            )
        terms = keep.tile([P, 4, BLOCKS], F32)
        nc.scalar.activation(
            out=terms[:, 3, :], in_=small_t[:, SLOTS, :], func=ACT.Identity, bias=0.5
        )
        h3_words = h3_rows[:].bitcast(F32)
        h3_t = psum.tile([P, PASSES, 2, B], F32, tag="bank")
        for c in range(PASSES):
            for u in range(2):
                nc.tensor.transpose(
                    h3_t[:, c, u, :],
                    h3_words[:, c * 2 * P + u : (c + 1) * 2 * P : 2],
                    ident_f32[:],
                )
        h3_grouped = keep.tile([P, PASSES, B, 2], F32, align_bytes=64)
        nc.scalar.copy(out=h3_grouped[:], in_=h3_t[:].rearrange("p c u b -> p c b u"))
        h3_codes = keep.tile([P, PASSES, B], U32, align_bytes=64)
        h3_scales = keep.tile([P, PASSES, B], U8, align_bytes=64)

        quantise_chunk(1, lower)
        quantise_chunk(1, upper)
        zxy = keep.tile([P, 3, BLOCKS], F32)
        nc.vector.scalar_tensor_tensor(
            out=zxy[:, 1:3, :], in0=trig[:, COS : SIN + 1, PH0, :], scalar=0.5,
            in1=twice(trig[:, SIN, TH0, :]), op0=ALU.mult, op1=ALU.mult,
        )
        from_z = keep.tile([P, 2, BLOCKS], F32)
        nc.vector.scalar_tensor_tensor(
            out=from_z[:], in0=trig[:, COS : SIN + 1, TH1, :], scalar=0.5,
            in1=twice(trig[:, COS, TH0, :]), op0=ALU.mult, op1=ALU.mult,
        )
        nc.vector.tensor_tensor(
            out=trig[:, COS, SLOTS : SLOTS + 2, :], in0=trig[:, COS::-1, PH1, :],
            in1=twice(trig[:, NSIN, TH2, :]), op=ALU.mult,
        )
        regroup_chunk(2)
        from_x = keep.tile([P, 2, BLOCKS], F32)
        nc.vector.tensor_tensor(
            out=from_x[:], in0=trig[:, NSIN : COS + 1, TH1, :], in1=twice(zxy[:, 1, :]),
            op=ALU.mult,
        )
        nc.vector.quantize_mx(
            out=h3_codes[:].rearrange("p c b -> p (c b)").bitcast(FP8X4),
            scales=h3_scales[:].rearrange("p c b -> p (c b)"),
            in_=h3_grouped[:].rearrange("p c b u -> p (c b u)").bitcast(BF16),
        )
        nc.vector.tensor_tensor(out=zxy[:, 0:2, :], in0=from_z[:], in1=from_x[:], op=ALU.add)
        quantise_chunk(2, lower)
        regroup_chunk(3)
        nc.vector.tensor_tensor(
            out=terms[:, 0:3, :], in0=trig[:, COS, TH2 : TH2 + 3, :], in1=zxy[:], op=ALU.mult
        )
        quantise_chunk(2, upper)
        bias = keep.tile([P, BLOCKS], F32)
        nc.vector.tensor_reduce(
            out=bias[:], in_=terms[:].rearrange("p r n -> p n r"), op=ALU.add,
            axis=mybir.AxisListType.X,
        )

        h4_t = [keep.tile([P, PACK, B], BF16, name="h4_t_%d" % g) for g in range(PASSES)]

        acc = [psum.tile([P, B], F32, tag="bank", name="acc_%d" % n) for n in range(BLOCKS)]

        def first_product(g, c):
            for t in range(UNITS):
                units = slice(t * P, (t + 1) * P)
                nc.tensor.matmul_mx(
                    out=acc[g * UNITS + t][:],
                    lhsT=cw_codes[:, g * PASSES + c, units].bitcast(FP8X4),
                    lhsT_scale=cw_scales[:, g * PASSES + c, units],
                    rhs=h3_codes[:, c, :].bitcast(FP8X4),
                    rhs_scale=h3_scales[:, c, :],
                    start=(c == 0),
                    stop=(c == PASSES - 1),
                )

        def tanh(g):
            for t in range(UNITS):
                n = g * UNITS + t
                nc.scalar.activation(
                    out=h4_t[g][:, t, :], in_=acc[n][:], func=ACT.Tanh, bias=bias[:, n : n + 1]
                )

        first_product(0, 0)
        first_product(0, 1)
        tanh(0)
        first_product(1, 0)
        quantise_chunk(3, lower)
        quantise_chunk(3, upper)
        first_product(1, 1)
        tanh(1)

        w3_grouped = keep.tile([P, PASSES, D_OUT, PACK], BF16, align_bytes=64)
        w3_codes = keep.tile([P, PASSES, D_OUT], U32, align_bytes=64)
        w3_scales = keep.tile([P, PASSES, D_OUT], U8, align_bytes=64)
        h4_grouped = keep.tile([P, PASSES, B, PACK], BF16, align_bytes=64)
        h4_codes = keep.tile([P, PASSES, B], U32, align_bytes=64)
        h4_scales = keep.tile([P, PASSES, B], U8, align_bytes=64)
        out_acc = psum.tile([B, D_OUT], F32, tag="bank")

        def quantise_h4(g):
            nc.vector.quantize_mx(
                out=h4_codes[:, g, :].bitcast(FP8X4),
                scales=h4_scales[:, g, :],
                in_=h4_grouped[:, g, :, :].rearrange("p b t -> p (b t)"),
            )

        def second_product(g):
            nc.tensor.matmul_mx(
                out=out_acc[:],
                lhsT=h4_codes[:, g, :].bitcast(FP8X4),
                lhsT_scale=h4_scales[:, g, :],
                rhs=w3_codes[:, g, :].bitcast(FP8X4),
                rhs_scale=w3_scales[:, g, :],
                start=(g == 0),
                stop=(g == PASSES - 1),
            )

        for g in range(PASSES):
            regroup(nc.vector.tensor_copy, w3_grouped[:, g, :, :], w3_rows[:, g, :, :])
        regroup(nc.vector.tensor_copy, h4_grouped[:, 0, :, :], h4_t[0][:])
        nc.vector.quantize_mx(
            out=w3_codes[:].rearrange("p g n -> p (g n)").bitcast(FP8X4),
            scales=w3_scales[:].rearrange("p g n -> p (g n)"),
            in_=w3_grouped[:].rearrange("p g n t -> p (g n t)"),
        )
        regroup(nc.vector.tensor_copy, h4_grouped[:, 1, :, :], h4_t[1][:])
        quantise_h4(0)
        second_product(0)
        quantise_h4(1)
        second_product(1)

        result = keep.tile([B, D_OUT], F32)
        halves = (slice(0, D_OUT // 2), slice(D_OUT // 2, D_OUT))
        for half in halves:
            nc.vector.tensor_tensor(
                out=result[:, half], in0=out_acc[:, half], in1=b3_all[:, half], op=ALU.add
            )
        for half in halves:
            nc.vector.tensor_scalar(
                out=result[:, half], in0=result[:, half], scalar1=0.0, scalar2=None, op0=ALU.max
            )
        nc.sync.dma_start(out=out, in_=result[:])
